import numpy as np
import ml_dtypes


def mxq(x, axis, fmt="e4m3"):
    dtype, down = {"e4m3": (ml_dtypes.float8_e4m3fn, 7), "e5m2": (ml_dtypes.float8_e5m2, 14)}[fmt]
    v = np.moveaxis(np.asarray(x, np.float32).astype(ml_dtypes.bfloat16).astype(np.float64), axis, -1)
    blocks = v.reshape(v.shape[:-1] + (-1, 32))
    amax = np.abs(blocks).max(-1, keepdims=True)
    byte = np.maximum(np.where(amax > 0, np.frexp(amax)[1] - 1 + 127, 0) - down, 1)
    scale = np.exp2(byte - 127.0)
    codes = (blocks / scale).astype(np.float32).astype(dtype).astype(np.float64)
    return np.moveaxis((codes * scale).reshape(v.shape), -1, axis)


WIDE = False


def mx_kscale(k):
    if not WIDE:
        return np.ones(k)
    levels = np.array([10, -10, 5, -5, 0])
    a = np.random.permutation(np.resize(levels, k // 512 * 4)).reshape(k // 512, 4)
    idx = np.arange(k)
    return np.exp2(a[idx // 512, idx % 128 // 32])


BF16 = ml_dtypes.bfloat16


def bf(x):
    return np.asarray(x, np.float32).astype(BF16)


def f64(x):
    return np.asarray(x).astype(np.float64)


E2M1 = np.array([0.0, 0.5, 1.0, 1.5, 2.0, 3.0, 4.0, 6.0, -0.0, -0.5, -1.0, -1.5, -2.0, -3.0, -4.0, -6.0])


def pack_weight(w, fmt):
    k, n = w.shape
    w = f64(bf(w)).reshape(k // 32, 32, n)
    amax = np.abs(w).max(1)
    if fmt == "e4m3":
        byte = np.frexp(amax)[1] - 1 + 127 - 7
    else:
        mant, ex = np.frexp(amax / 6.0)
        byte = np.where(mant > 0.5, ex, ex - 1) + 127
    byte = np.clip(np.where(amax > 0, byte, 1), 1, 254)
    scaled = (w * np.exp2(127.0 - byte)[:, None, :]).reshape(k, n).astype(np.float32)
    by_word = np.ascontiguousarray(scaled.reshape(k // 512, 128, 4, n).transpose(0, 1, 3, 2))
    if fmt == "e4m3":
        words = by_word.astype(ml_dtypes.float8_e4m3fn).view(np.uint8)
    else:
        c = by_word.astype(ml_dtypes.float4_e2m1fn).view(np.uint8) & 0xF
        words = c[..., 0::2] | (c[..., 1::2] << 4)
    return np.ascontiguousarray(words), np.ascontiguousarray(byte.astype(np.uint8).reshape(k // 512, 16, n))


def unpack_weight(words, scales, fmt):
    g, p, n, _ = words.shape
    if fmt == "e4m3":
        vals = np.ascontiguousarray(words).view(ml_dtypes.float8_e4m3fn).astype(np.float64)
    else:
        nib = np.empty((g, p, n, 4), np.uint8)
        nib[..., 0::2] = words & 0xF
        nib[..., 1::2] = words >> 4
        vals = E2M1[nib]
    vals = vals * np.repeat(np.exp2(scales.astype(np.float64) - 127.0), 8, axis=1)[..., None]
    return vals.transpose(0, 1, 3, 2).reshape(g * 512, n)


B, S, DIM, H, DH, DV, R = 2, 64, 1024, 16, 64, 64, 8192
EPS = 1e-6
N = H * (DH + DV)
FMT = "e4m3"


def rmsnorm(c, w):
    norm = np.mean(c * c, axis=-1, keepdims=True)
    return w * (c * (1.0 / np.sqrt(norm + EPS)))


def setup_inputs():
    s, t = mx_kscale(DIM), mx_kscale(R)
    x = bf(np.random.standard_normal((B, S, DIM)) * s)
    wa = np.random.standard_normal((R, DIM)) / np.sqrt(DIM) / s[None, :]
    wa_words, wa_scales = pack_weight(np.ascontiguousarray(wa.T), FMT)
    wkv_a_b = bf(np.random.standard_normal(R) * 0.3)
    kv_norm_w = bf((1.0 + 0.1 * np.random.standard_normal(R)) * t)
    wb = np.random.standard_normal((N, R)) / np.sqrt(R) / t[None, :]
    wb_words, wb_scales = pack_weight(np.ascontiguousarray(wb.T), FMT)
    wkv_b_b = bf(np.random.standard_normal(N) * 0.3)
    return {"x": x,
            "wkv_a_w_words": wa_words,
            "wkv_a_w_scales": wa_scales,
            "wkv_a_b": wkv_a_b,
            "kv_norm_w": kv_norm_w,
            "wkv_b_w_words": wb_words,
            "wkv_b_w_scales": wb_scales,
            "wkv_b_b": wkv_b_b}


def reference(x, wkv_a_w_words, wkv_a_w_scales, wkv_a_b, kv_norm_w, wkv_b_w_words, wkv_b_w_scales, wkv_b_b):
    c = (mxq(f64(x), 2, "e4m3") @ unpack_weight(wkv_a_w_words, wkv_a_w_scales, FMT)) + f64(wkv_a_b)
    kv_c = rmsnorm(c, f64(kv_norm_w))
    kv = (mxq(kv_c, 2, "e4m3") @ unpack_weight(wkv_b_w_words, wkv_b_w_scales, FMT)) + f64(wkv_b_b)
    kv = kv.reshape(B, S, H, DH + DV)
    return kv[..., :DH], kv[..., DH:]

@@ -1,0 +1,262 @@
+from contextlib import ExitStack
+
+import concourse.mybir as mybir
+from concourse.masks import make_identity
+
+F32 = mybir.dt.float32
+BF16 = mybir.dt.bfloat16
+I32 = mybir.dt.int32
+U32 = mybir.dt.uint32
+U8 = mybir.dt.uint8
+FP8X4 = mybir.dt.float8_e4m3fn_x4
+ALU = mybir.AluOpType
+ACT = mybir.ActivationFunctionType
+AXIS = mybir.AxisListType
+
+P = 128
+PACK = 4
+K_PASS = P * PACK
+DIM = 1024
+LATENT = 8192
+KV = 2048
+HEADS = 16
+HEAD_DIM = 64
+EPS = 1e-6
+A_PASSES = DIM // K_PASS
+B_PASSES = LATENT // K_PASS
+N_TILE = 512
+CHUNK = 2048
+TILES_PER_CHUNK = CHUNK // N_TILE
+QUADRANT = 32
+SHARED = 4
+WORD_BUFS = 16
+GROUP_RUN = 4
+
+ROW_A_BIAS = 0
+ROW_GAIN = 16
+ROW_B_BIAS = 32
+
+FLOPS = 2 * P * (DIM * LATENT + LATENT * KV)
+
+
+def load_shared_planes(nc, planes, scale_rows):
+    for quad in range(4):
+        first = QUADRANT * quad
+        nc.sync.dma_start(
+            out=planes[first : first + 4 * SHARED, :].bitcast(I32),
+            in_=scale_rows[:, 4 * quad : 4 * quad + 4, :].bitcast(I32),
+        )
+
+
+def load_words(nc, pool, dram_bytes):
+    words = pool.tile([P, CHUNK], U32, tag="words", align_bytes=64)
+    nc.sync.dma_start(out=words[:].bitcast(I32), in_=dram_bytes.bitcast(I32))
+    return words
+
+
+def broadcast_rows(nc, psum, ident_bf16, rows, first_row, dest):
+    for j in range(0, dest.shape[1], 2):
+        bank = psum.tile([P, 2, N_TILE], BF16, tag="plain")
+        for i in range(2):
+            row = first_row + j + i
+            nc.tensor.matmul(
+                out=bank[:, i, :],
+                lhsT=ident_bf16[:, row : row + 1].to_broadcast([P, P]),
+                rhs=rows,
+                start=True,
+                stop=True,
+            )
+        if j % 4 == 0:
+            nc.vector.tensor_copy(out=dest[:, j : j + 2, :], in_=bank[:])
+        else:
+            nc.scalar.copy(out=dest[:, j : j + 2, :], in_=bank[:])
+
+
+def tile_mla_pa_k_kernel(
+    tc,
+    x,
+    wkv_a_w_words,
+    wkv_a_w_scales,
+    wkv_a_b,
+    kv_norm_w,
+    wkv_b_w_words,
+    wkv_b_w_scales,
+    wkv_b_b,
+    out_0,
+    out_1,
+):
+    nc = tc.nc
+    with ExitStack() as ctx:
+        const = ctx.enter_context(tc.tile_pool(name="const", bufs=1))
+        word_pool = ctx.enter_context(tc.tile_pool(name="word_pool", bufs=WORD_BUFS))
+        work = ctx.enter_context(tc.tile_pool(name="work", bufs=2))
+        psum = ctx.enter_context(tc.psum_pool(name="psum", bufs=4))
+
+        rows = const.tile([P, N_TILE], BF16)
+        a_planes = const.tile([P, A_PASSES, CHUNK], U8, align_bytes=64)
+        b_planes = const.tile([P, B_PASSES // SHARED, KV], U8, align_bytes=64)
+        nc.vector.memset(rows[:], 0.0)
+        nc.vector.memset(a_planes[:].bitcast(I32), 0)
+        nc.vector.memset(b_planes[:].bitcast(I32), 0)
+
+        ident_f32 = const.tile([P, P], F32)
+        ident_bf16 = const.tile([P, P], BF16)
+        make_identity(nc, ident_f32[:])
+        make_identity(nc, ident_bf16[:])
+
+        x_sb = const.tile([P, DIM], BF16)
+        nc.sync.dma_start(out=x_sb[:], in_=x.flatten_outer_dims())
+        nc.scalar.dma_start(
+            out=rows[ROW_A_BIAS : ROW_A_BIAS + LATENT // N_TILE, :],
+            in_=wkv_a_b.rearrange("(r c) -> r c", c=N_TILE),
+        )
+        nc.scalar.dma_start(
+            out=rows[ROW_GAIN : ROW_GAIN + LATENT // N_TILE, :],
+            in_=kv_norm_w.rearrange("(r c) -> r c", c=N_TILE),
+        )
+        nc.scalar.dma_start(
+            out=rows[ROW_B_BIAS : ROW_B_BIAS + KV // N_TILE, :],
+            in_=wkv_b_b.rearrange("(r c) -> r c", c=N_TILE),
+        )
+        for g in range(A_PASSES):
+            load_shared_planes(
+                nc, a_planes[:, g, :], wkv_a_w_scales[g].rearrange("q (j c) -> j q c", j=SHARED)
+            )
+
+        x_words = x_sb[:].bitcast(F32)
+        x_t = psum.tile([P, A_PASSES, 2, P], F32, tag="plain")
+        for g in range(A_PASSES):
+            for u in range(2):
+                nc.tensor.transpose(
+                    x_t[:, g, u, :],
+                    x_words[:, (K_PASS // 2) * g + u : (K_PASS // 2) * (g + 1) : 2],
+                    ident_f32[:],
+                )
+        x_grouped = const.tile([P, A_PASSES * P * PACK], BF16, align_bytes=64)
+        nc.vector.tensor_copy(
+            out=x_grouped[:].bitcast(F32).rearrange("p (g m u) -> p g m u", g=A_PASSES, u=2),
+            in_=x_t[:].rearrange("p g u m -> p g m u"),
+        )
+        x_codes = const.tile([P, A_PASSES * P], U32, align_bytes=64)
+        x_scales = const.tile([P, A_PASSES * P], U8, align_bytes=64)
+        nc.vector.quantize_mx(out=x_codes[:].bitcast(FP8X4), scales=x_scales[:], in_=x_grouped[:])
+
+        rows_tp = const.tile([P, PACK, P], BF16)
+        nc.vector.tensor_copy(out=rows_tp[:], in_=rows[:].rearrange("r (p t) -> r t p", t=PACK))
+        a_bias = const.tile([P, B_PASSES, N_TILE], BF16)
+        broadcast_rows(
+            nc, psum, ident_bf16, rows_tp[:].rearrange("r t p -> r (t p)"), ROW_A_BIAS, a_bias
+        )
+        rows_t = psum.tile([P, PACK, P], BF16, tag="plain")
+        for t in range(PACK):
+            nc.tensor.transpose(rows_t[:, t, :], rows_tp[:, t, :], ident_bf16[:])
+        gain = const.tile([P, B_PASSES, PACK], F32)
+        nc.vector.tensor_copy(
+            out=gain[:], in_=rows_t[:, :, ROW_GAIN : ROW_GAIN + B_PASSES].rearrange("p t g -> p g t")
+        )
+        b_bias = const.tile([P, KV // N_TILE, N_TILE], BF16)
+        broadcast_rows(nc, psum, ident_bf16, rows[:], ROW_B_BIAS, b_bias)
+
+        c_sb = const.tile([P, B_PASSES, PACK, P], F32)
+        sum_sq = const.tile([P, B_PASSES], F32)
+        for j in range(LATENT // CHUNK):
+            a_words = []
+            for g in range(A_PASSES):
+                flat = wkv_a_w_words[g].rearrange("p n t -> p (n t)")
+                a_words.append(load_words(nc, word_pool, flat[:, PACK * CHUNK * j : PACK * CHUNK * (j + 1)]))
+            for i in range(TILES_PER_CHUNK):
+                cols = slice(N_TILE * i, N_TILE * (i + 1))
+                bank_no = TILES_PER_CHUNK * j + i
+                c_ps = psum.tile([P, N_TILE], F32, tag="mx")
+                for g in range(A_PASSES):
+                    nc.tensor.matmul_mx(
+                        out=c_ps[:],
+                        lhsT=x_codes[:, P * g : P * (g + 1)].bitcast(FP8X4),
+                        lhsT_scale=x_scales[:, P * g : P * (g + 1)],
+                        rhs=a_words[g][:, cols].bitcast(FP8X4),
+                        rhs_scale=a_planes[4 * j : P, g, cols],
+                        start=(g == 0),
+                        stop=(g == A_PASSES - 1),
+                    )
+                nc.vector.tensor_tensor(
+                    out=c_sb[:, bank_no],
+                    in0=c_ps[:].rearrange("m (p t) -> m t p", t=PACK),
+                    in1=a_bias[:, bank_no, :].rearrange("m (t p) -> m t p", t=PACK),
+                    op=ALU.add,
+                )
+                squares = work.tile([P, PACK, P], BF16)
+                nc.scalar.activation(
+                    out=squares[:],
+                    in_=c_sb[:, bank_no],
+                    func=ACT.Square,
+                    accum_out=sum_sq[:, bank_no : bank_no + 1],
+                )
+
+        for block in range(B_PASSES // SHARED):
+            load_shared_planes(
+                nc, b_planes[:, block, :], wkv_b_w_scales[SHARED * block : SHARED * (block + 1)]
+            )
+        b_words = []
+        for g in range(B_PASSES):
+            b_words.append(load_words(nc, word_pool, wkv_b_w_words[g].rearrange("p n t -> p (n t)")))
+
+        total = const.tile([P, 1], F32)
+        mean_eps = const.tile([P, 1], F32)
+        rms = const.tile([P, 1], F32)
+        inv_rms = const.tile([P, 1], F32)
+        nc.vector.reduce_sum(out=total[:], in_=sum_sq[:], axis=AXIS.X)
+        nc.vector.tensor_scalar(
+            out=mean_eps[:], in0=total[:], scalar1=1.0 / LATENT, scalar2=EPS, op0=ALU.mult, op1=ALU.add
+        )
+        nc.scalar.sqrt(out=rms[:], in_=mean_eps[:])
+        nc.vector.reciprocal(out=inv_rms[:], in_=rms[:])
+
+        kv_codes = const.tile([P, B_PASSES * P], U32, align_bytes=64)
+        kv_scales = const.tile([P, B_PASSES * P], U8, align_bytes=64)
+        kv_ps = [psum.tile([P, N_TILE], F32, tag="mx", name="kv_ps%d" % i) for i in range(KV // N_TILE)]
+        for first in range(0, B_PASSES, GROUP_RUN):
+            run = slice(first, first + GROUP_RUN)
+            nc.scalar.activation(out=c_sb[:, run], in_=c_sb[:, run], func=ACT.Copy, scale=inv_rms[:, 0:1])
+            kv_grouped = work.tile([P, GROUP_RUN, P, PACK], BF16, align_bytes=64)
+            for g in range(first, first + GROUP_RUN):
+                c_t = psum.tile([P, PACK, P], F32, tag="plain")
+                for t in range(PACK):
+                    nc.tensor.transpose(c_t[:, t, :], c_sb[:, g, t, :], ident_f32[:])
+                nc.vector.tensor_tensor(
+                    out=kv_grouped[:, g - first],
+                    in0=c_t[:].rearrange("p t m -> p m t"),
+                    in1=gain[:, g, :].unsqueeze(1).to_broadcast([P, P, PACK]),
+                    op=ALU.mult,
+                )
+            nc.vector.quantize_mx(
+                out=kv_codes[:, P * first : P * (first + GROUP_RUN)].bitcast(FP8X4),
+                scales=kv_scales[:, P * first : P * (first + GROUP_RUN)],
+                in_=kv_grouped[:].rearrange("p g m t -> p (g m t)"),
+            )
+            for g in range(first, first + GROUP_RUN):
+                for i in range(KV // N_TILE):
+                    cols = slice(N_TILE * i, N_TILE * (i + 1))
+                    nc.tensor.matmul_mx(
+                        out=kv_ps[i][:],
+                        lhsT=kv_codes[:, P * g : P * (g + 1)].bitcast(FP8X4),
+                        lhsT_scale=kv_scales[:, P * g : P * (g + 1)],
+                        rhs=b_words[g][:, cols].bitcast(FP8X4),
+                        rhs_scale=b_planes[4 * (g % SHARED) : P, g // SHARED, cols],
+                        start=(g == 0),
+                        stop=(g == B_PASSES - 1),
+                    )
+
+        kv_out = const.tile([P, 2, HEADS, HEAD_DIM], F32)
+        k_rows = out_0.rearrange("b s h d -> (b s) h d")
+        v_rows = out_1.rearrange("b s h d -> (b s) h d")
+        heads_per_bank = N_TILE // (2 * HEAD_DIM)
+        for i in range(KV // N_TILE):
+            heads = slice(heads_per_bank * i, heads_per_bank * (i + 1))
+            nc.vector.tensor_tensor(
+                out=kv_out[:, :, heads, :],
+                in0=kv_ps[i][:].rearrange("m (h s d) -> m s h d", s=2, d=HEAD_DIM),
+                in1=b_bias[:, i, :].rearrange("m (h s d) -> m s h d", s=2, d=HEAD_DIM),
+                op=ALU.add,
+            )
+            nc.sync.dma_start(out=k_rows[:, heads, :], in_=kv_out[:, 0, heads, :])
+            nc.sync.dma_start(out=v_rows[:, heads, :], in_=kv_out[:, 1, heads, :])

@@ -19,7 +19,6 @@ K_PASS = P * PACK
 DIM = 1024
 LATENT = 8192
 KV = 2048
-HEADS = 16
 HEAD_DIM = 64
 EPS = 1e-6
 A_PASSES = DIM // K_PASS
@@ -31,6 +30,7 @@ QUADRANT = 32
 SHARED = 4
 WORD_BUFS = 16
 GROUP_RUN = 4
+BANK_BUFS = 6
 
 ROW_A_BIAS = 0
 ROW_GAIN = 16
@@ -90,6 +90,7 @@ def tile_mla_pa_k_kernel(
         const = ctx.enter_context(tc.tile_pool(name="const", bufs=1))
         word_pool = ctx.enter_context(tc.tile_pool(name="word_pool", bufs=WORD_BUFS))
         work = ctx.enter_context(tc.tile_pool(name="work", bufs=2))
+        banks = ctx.enter_context(tc.tile_pool(name="banks", bufs=BANK_BUFS))
         psum = ctx.enter_context(tc.psum_pool(name="psum", bufs=4))
 
         rows = const.tile([P, N_TILE], BF16)
@@ -157,20 +158,19 @@ def tile_mla_pa_k_kernel(
         b_bias = const.tile([P, KV // N_TILE, N_TILE], BF16)
         broadcast_rows(nc, psum, ident_bf16, rows[:], ROW_B_BIAS, b_bias)
 
-        c_sb = const.tile([P, B_PASSES, PACK, P], F32)
+        c_gain = const.tile([P, B_PASSES, P, PACK], F32)
         sum_sq = const.tile([P, B_PASSES], F32)
         for j in range(LATENT // CHUNK):
             a_words = []
             for g in range(A_PASSES):
                 flat = wkv_a_w_words[g].rearrange("p n t -> p (n t)")
                 a_words.append(load_words(nc, word_pool, flat[:, PACK * CHUNK * j : PACK * CHUNK * (j + 1)]))
-            for i in range(TILES_PER_CHUNK):
-                cols = slice(N_TILE * i, N_TILE * (i + 1))
-                bank_no = TILES_PER_CHUNK * j + i
-                c_ps = psum.tile([P, N_TILE], F32, tag="mx")
-                for g in range(A_PASSES):
+            c_ps = [psum.tile([P, N_TILE], F32, tag="mx", name="c_ps%d" % i) for i in range(TILES_PER_CHUNK)]
+            for g in range(A_PASSES):
+                for i in range(TILES_PER_CHUNK):
+                    cols = slice(N_TILE * i, N_TILE * (i + 1))
                     nc.tensor.matmul_mx(
-                        out=c_ps[:],
+                        out=c_ps[i][:],
                         lhsT=x_codes[:, P * g : P * (g + 1)].bitcast(FP8X4),
                         lhsT_scale=x_scales[:, P * g : P * (g + 1)],
                         rhs=a_words[g][:, cols].bitcast(FP8X4),
@@ -178,18 +178,31 @@ def tile_mla_pa_k_kernel(
                         start=(g == 0),
                         stop=(g == A_PASSES - 1),
                     )
+            c_sb = []
+            for i in range(TILES_PER_CHUNK):
+                bank_no = TILES_PER_CHUNK * j + i
+                c_bank = banks.tile([P, PACK, P], F32, tag="bank")
                 nc.vector.tensor_tensor(
-                    out=c_sb[:, bank_no],
-                    in0=c_ps[:].rearrange("m (p t) -> m t p", t=PACK),
+                    out=c_bank[:],
+                    in0=c_ps[i][:].rearrange("m (p t) -> m t p", t=PACK),
                     in1=a_bias[:, bank_no, :].rearrange("m (t p) -> m t p", t=PACK),
                     op=ALU.add,
                 )
                 squares = work.tile([P, PACK, P], BF16)
                 nc.scalar.activation(
-                    out=squares[:],
-                    in_=c_sb[:, bank_no],
-                    func=ACT.Square,
-                    accum_out=sum_sq[:, bank_no : bank_no + 1],
+                    out=squares[:], in_=c_bank[:], func=ACT.Square, accum_out=sum_sq[:, bank_no : bank_no + 1]
+                )
+                c_sb.append(c_bank)
+            for i in range(TILES_PER_CHUNK):
+                bank_no = TILES_PER_CHUNK * j + i
+                c_t = psum.tile([P, PACK, P], F32, tag="plain")
+                for t in range(PACK):
+                    nc.tensor.transpose(c_t[:, t, :], c_sb[i][:, t, :], ident_f32[:])
+                nc.vector.tensor_tensor(
+                    out=c_gain[:, bank_no],
+                    in0=c_t[:].rearrange("p t m -> p m t"),
+                    in1=gain[:, bank_no, :].unsqueeze(1).to_broadcast([P, P, PACK]),
+                    op=ALU.mult,
                 )
 
         for block in range(B_PASSES // SHARED):
@@ -210,24 +223,22 @@ def tile_mla_pa_k_kernel(
         )
         nc.scalar.sqrt(out=rms[:], in_=mean_eps[:])
         nc.vector.reciprocal(out=inv_rms[:], in_=rms[:])
+        inv_rms_rep = const.tile([P, P], F32)
+        nc.vector.tensor_copy(out=inv_rms_rep[:], in_=inv_rms[:, 0:1].to_broadcast([P, P]))
+        inv_rms_t = psum.tile([P, P], F32, tag="plain")
+        nc.tensor.transpose(inv_rms_t[:], inv_rms_rep[:], ident_f32[:])
 
         kv_codes = const.tile([P, B_PASSES * P], U32, align_bytes=64)
         kv_scales = const.tile([P, B_PASSES * P], U8, align_bytes=64)
         kv_ps = [psum.tile([P, N_TILE], F32, tag="mx", name="kv_ps%d" % i) for i in range(KV // N_TILE)]
         for first in range(0, B_PASSES, GROUP_RUN):
-            run = slice(first, first + GROUP_RUN)
-            nc.scalar.activation(out=c_sb[:, run], in_=c_sb[:, run], func=ACT.Copy, scale=inv_rms[:, 0:1])
             kv_grouped = work.tile([P, GROUP_RUN, P, PACK], BF16, align_bytes=64)
-            for g in range(first, first + GROUP_RUN):
-                c_t = psum.tile([P, PACK, P], F32, tag="plain")
-                for t in range(PACK):
-                    nc.tensor.transpose(c_t[:, t, :], c_sb[:, g, t, :], ident_f32[:])
-                nc.vector.tensor_tensor(
-                    out=kv_grouped[:, g - first],
-                    in0=c_t[:].rearrange("p t m -> p m t"),
-                    in1=gain[:, g, :].unsqueeze(1).to_broadcast([P, P, PACK]),
-                    op=ALU.mult,
-                )
+            nc.vector.tensor_tensor(
+                out=kv_grouped[:],
+                in0=c_gain[:, first : first + GROUP_RUN],
+                in1=inv_rms_t[:].unsqueeze(1).unsqueeze(3).to_broadcast([P, GROUP_RUN, P, PACK]),
+                op=ALU.mult,
+            )
             nc.vector.quantize_mx(
                 out=kv_codes[:, P * first : P * (first + GROUP_RUN)].bitcast(FP8X4),
                 scales=kv_scales[:, P * first : P * (first + GROUP_RUN)],
@@ -246,17 +257,17 @@ def tile_mla_pa_k_kernel(
                         stop=(g == B_PASSES - 1),
                     )
 
-        kv_out = const.tile([P, 2, HEADS, HEAD_DIM], F32)
         k_rows = out_0.rearrange("b s h d -> (b s) h d")
         v_rows = out_1.rearrange("b s h d -> (b s) h d")
         heads_per_bank = N_TILE // (2 * HEAD_DIM)
         for i in range(KV // N_TILE):
             heads = slice(heads_per_bank * i, heads_per_bank * (i + 1))
+            kv_out = banks.tile([P, 2, heads_per_bank, HEAD_DIM], F32, tag="bank")
             nc.vector.tensor_tensor(
-                out=kv_out[:, :, heads, :],
+                out=kv_out[:],
                 in0=kv_ps[i][:].rearrange("m (h s d) -> m s h d", s=2, d=HEAD_DIM),
                 in1=b_bias[:, i, :].rearrange("m (h s d) -> m s h d", s=2, d=HEAD_DIM),
                 op=ALU.add,
             )
-            nc.sync.dma_start(out=k_rows[:, heads, :], in_=kv_out[:, 0, heads, :])
-            nc.sync.dma_start(out=v_rows[:, heads, :], in_=kv_out[:, 1, heads, :])
+            nc.sync.dma_start(out=k_rows[:, heads, :], in_=kv_out[:, 0])
+            nc.sync.dma_start(out=v_rows[:, heads, :], in_=kv_out[:, 1])

@@ -39,12 +39,12 @@ ROW_B_BIAS = 32
 FLOPS = 2 * P * (DIM * LATENT + LATENT * KV)
 
 
-def load_shared_planes(nc, planes, scale_rows):
+def load_shared_planes(queue, word, planes, scale_rows):
     for quad in range(4):
         first = QUADRANT * quad
-        nc.sync.dma_start(
-            out=planes[first : first + 4 * SHARED, :].bitcast(I32),
-            in_=scale_rows[:, 4 * quad : 4 * quad + 4, :].bitcast(I32),
+        queue.dma_start(
+            out=planes[first : first + 4 * SHARED, :].bitcast(word),
+            in_=scale_rows[:, 4 * quad : 4 * quad + 4, :].bitcast(word),
         )
 
 
@@ -105,24 +105,33 @@ def tile_mla_pa_k_kernel(
         make_identity(nc, ident_f32[:])
         make_identity(nc, ident_bf16[:])
 
-        x_sb = const.tile([P, DIM], BF16)
-        nc.sync.dma_start(out=x_sb[:], in_=x.flatten_outer_dims())
-        nc.scalar.dma_start(
+        nc.gpsimd.dma_start(
             out=rows[ROW_A_BIAS : ROW_A_BIAS + LATENT // N_TILE, :],
             in_=wkv_a_b.rearrange("(r c) -> r c", c=N_TILE),
         )
-        nc.scalar.dma_start(
+        nc.gpsimd.dma_start(
             out=rows[ROW_GAIN : ROW_GAIN + LATENT // N_TILE, :],
             in_=kv_norm_w.rearrange("(r c) -> r c", c=N_TILE),
         )
-        nc.scalar.dma_start(
+        nc.gpsimd.dma_start(
             out=rows[ROW_B_BIAS : ROW_B_BIAS + KV // N_TILE, :],
             in_=wkv_b_b.rearrange("(r c) -> r c", c=N_TILE),
         )
-        for g in range(A_PASSES):
+        for block in range(B_PASSES // SHARED):
             load_shared_planes(
-                nc, a_planes[:, g, :], wkv_a_w_scales[g].rearrange("q (j c) -> j q c", j=SHARED)
+                nc.gpsimd, F32, b_planes[:, block, :], wkv_b_w_scales[SHARED * block : SHARED * (block + 1)]
             )
+        x_sb = const.tile([P, DIM], BF16)
+        nc.sync.dma_start(out=x_sb[:], in_=x.flatten_outer_dims())
+        a_words = {}
+        for j in range(LATENT // CHUNK):
+            for g in range(A_PASSES):
+                if j == 0:
+                    load_shared_planes(
+                        nc.sync, I32, a_planes[:, g, :], wkv_a_w_scales[g].rearrange("q (j c) -> j q c", j=SHARED)
+                    )
+                flat = wkv_a_w_words[g].rearrange("p n t -> p (n t)")
+                a_words[(j, g)] = load_words(nc, word_pool, flat[:, PACK * CHUNK * j : PACK * CHUNK * (j + 1)])
 
         x_words = x_sb[:].bitcast(F32)
         x_t = psum.tile([P, A_PASSES, 2, P], F32, tag="plain")
@@ -161,10 +170,6 @@ def tile_mla_pa_k_kernel(
         c_gain = const.tile([P, B_PASSES, P, PACK], F32)
         sum_sq = const.tile([P, B_PASSES], F32)
         for j in range(LATENT // CHUNK):
-            a_words = []
-            for g in range(A_PASSES):
-                flat = wkv_a_w_words[g].rearrange("p n t -> p (n t)")
-                a_words.append(load_words(nc, word_pool, flat[:, PACK * CHUNK * j : PACK * CHUNK * (j + 1)]))
             c_ps = [psum.tile([P, N_TILE], F32, tag="mx", name="c_ps%d" % i) for i in range(TILES_PER_CHUNK)]
             for g in range(A_PASSES):
                 for i in range(TILES_PER_CHUNK):
@@ -173,7 +178,7 @@ def tile_mla_pa_k_kernel(
                         out=c_ps[i][:],
                         lhsT=x_codes[:, P * g : P * (g + 1)].bitcast(FP8X4),
                         lhsT_scale=x_scales[:, P * g : P * (g + 1)],
-                        rhs=a_words[g][:, cols].bitcast(FP8X4),
+                        rhs=a_words[(j, g)][:, cols].bitcast(FP8X4),
                         rhs_scale=a_planes[4 * j : P, g, cols],
                         start=(g == 0),
                         stop=(g == A_PASSES - 1),
@@ -205,10 +210,6 @@ def tile_mla_pa_k_kernel(
                     op=ALU.mult,
                 )
 
-        for block in range(B_PASSES // SHARED):
-            load_shared_planes(
-                nc, b_planes[:, block, :], wkv_b_w_scales[SHARED * block : SHARED * (block + 1)]
-            )
         b_words = []
         for g in range(B_PASSES):
             b_words.append(load_words(nc, word_pool, wkv_b_w_words[g].rearrange("p n t -> p (n t)")))

@@ -105,15 +105,15 @@ def tile_mla_pa_k_kernel(
         make_identity(nc, ident_f32[:])
         make_identity(nc, ident_bf16[:])
 
-        nc.gpsimd.dma_start(
+        nc.scalar.dma_start(
             out=rows[ROW_A_BIAS : ROW_A_BIAS + LATENT // N_TILE, :],
             in_=wkv_a_b.rearrange("(r c) -> r c", c=N_TILE),
         )
-        nc.gpsimd.dma_start(
+        nc.scalar.dma_start(
             out=rows[ROW_GAIN : ROW_GAIN + LATENT // N_TILE, :],
             in_=kv_norm_w.rearrange("(r c) -> r c", c=N_TILE),
         )
-        nc.gpsimd.dma_start(
+        nc.scalar.dma_start(
             out=rows[ROW_B_BIAS : ROW_B_BIAS + KV // N_TILE, :],
             in_=wkv_b_b.rearrange("(r c) -> r c", c=N_TILE),
         )
@@ -164,8 +164,6 @@ def tile_mla_pa_k_kernel(
         nc.vector.tensor_copy(
             out=gain[:], in_=rows_t[:, :, ROW_GAIN : ROW_GAIN + B_PASSES].rearrange("p t g -> p g t")
         )
-        b_bias = const.tile([P, KV // N_TILE, N_TILE], BF16)
-        broadcast_rows(nc, psum, ident_bf16, rows[:], ROW_B_BIAS, b_bias)
 
         c_gain = const.tile([P, B_PASSES, P, PACK], F32)
         sum_sq = const.tile([P, B_PASSES], F32)
@@ -228,6 +226,9 @@ def tile_mla_pa_k_kernel(
         nc.vector.tensor_copy(out=inv_rms_rep[:], in_=inv_rms[:, 0:1].to_broadcast([P, P]))
         inv_rms_t = psum.tile([P, P], F32, tag="plain")
         nc.tensor.transpose(inv_rms_t[:], inv_rms_rep[:], ident_f32[:])
+
+        b_bias = const.tile([P, KV // N_TILE, N_TILE], BF16)
+        broadcast_rows(nc, psum, ident_bf16, rows[:], ROW_B_BIAS, b_bias)
 
         kv_codes = const.tile([P, B_PASSES * P], U32, align_bytes=64)
         kv_scales = const.tile([P, B_PASSES * P], U8, align_bytes=64)

@@ -26,9 +26,11 @@ B_PASSES = LATENT // K_PASS
 N_TILE = 512
 CHUNK = 2048
 TILES_PER_CHUNK = CHUNK // N_TILE
+A_LOAD = 4096
+B_LOAD = 4
 QUADRANT = 32
 SHARED = 4
-WORD_BUFS = 16
+WORD_BUFS = 4
 GROUP_RUN = 4
 BANK_BUFS = 6
 
@@ -46,12 +48,6 @@ def load_shared_planes(queue, word, planes, scale_rows):
             out=planes[first : first + 4 * SHARED, :].bitcast(word),
             in_=scale_rows[:, 4 * quad : 4 * quad + 4, :].bitcast(word),
         )
-
-
-def load_words(nc, pool, dram_bytes):
-    words = pool.tile([P, CHUNK], U32, tag="words", align_bytes=64)
-    nc.sync.dma_start(out=words[:].bitcast(I32), in_=dram_bytes.bitcast(I32))
-    return words
 
 
 def broadcast_rows(nc, psum, ident_bf16, rows, first_row, dest):
@@ -123,15 +119,20 @@ def tile_mla_pa_k_kernel(
             )
         x_sb = const.tile([P, DIM], BF16)
         nc.sync.dma_start(out=x_sb[:], in_=x.flatten_outer_dims())
-        a_words = {}
-        for j in range(LATENT // CHUNK):
+        a_words = []
+        for h in range(LATENT // A_LOAD):
+            words = word_pool.tile([P, A_PASSES, A_LOAD], U32, tag="words", align_bytes=64)
             for g in range(A_PASSES):
-                if j == 0:
+                if h == 0:
                     load_shared_planes(
                         nc.sync, I32, a_planes[:, g, :], wkv_a_w_scales[g].rearrange("q (j c) -> j q c", j=SHARED)
                     )
                 flat = wkv_a_w_words[g].rearrange("p n t -> p (n t)")
-                a_words[(j, g)] = load_words(nc, word_pool, flat[:, PACK * CHUNK * j : PACK * CHUNK * (j + 1)])
+                nc.sync.dma_start(
+                    out=words[:, g, :].bitcast(I32),
+                    in_=flat[:, PACK * A_LOAD * h : PACK * A_LOAD * (h + 1)].bitcast(I32),
+                )
+            a_words.append(words)
 
         x_words = x_sb[:].bitcast(F32)
         x_t = psum.tile([P, A_PASSES, 2, P], F32, tag="plain")
@@ -172,11 +173,13 @@ def tile_mla_pa_k_kernel(
             for g in range(A_PASSES):
                 for i in range(TILES_PER_CHUNK):
                     cols = slice(N_TILE * i, N_TILE * (i + 1))
+                    first_word = (CHUNK * j) % A_LOAD + N_TILE * i
+                    word_cols = slice(first_word, first_word + N_TILE)
                     nc.tensor.matmul_mx(
                         out=c_ps[i][:],
                         lhsT=x_codes[:, P * g : P * (g + 1)].bitcast(FP8X4),
                         lhsT_scale=x_scales[:, P * g : P * (g + 1)],
-                        rhs=a_words[(j, g)][:, cols].bitcast(FP8X4),
+                        rhs=a_words[CHUNK * j // A_LOAD][:, g, word_cols].bitcast(FP8X4),
                         rhs_scale=a_planes[4 * j : P, g, cols],
                         start=(g == 0),
                         stop=(g == A_PASSES - 1),
@@ -209,8 +212,15 @@ def tile_mla_pa_k_kernel(
                 )
 
         b_words = []
-        for g in range(B_PASSES):
-            b_words.append(load_words(nc, word_pool, wkv_b_w_words[g].rearrange("p n t -> p (n t)")))
+        for first in range(0, B_PASSES, B_LOAD):
+            words = word_pool.tile([P, B_LOAD, KV], U32, tag="words", align_bytes=64)
+            step = B_LOAD if first + B_LOAD < B_PASSES else 1
+            for k in range(0, B_LOAD, step):
+                nc.sync.dma_start(
+                    out=words[:, k : k + step, :].bitcast(I32),
+                    in_=wkv_b_w_words[first + k : first + k + step].rearrange("g p n t -> p g (n t)").bitcast(I32),
+                )
+            b_words.append(words)
 
         total = const.tile([P, 1], F32)
         mean_eps = const.tile([P, 1], F32)
@@ -253,7 +263,7 @@ def tile_mla_pa_k_kernel(
                         out=kv_ps[i][:],
                         lhsT=kv_codes[:, P * g : P * (g + 1)].bitcast(FP8X4),
                         lhsT_scale=kv_scales[:, P * g : P * (g + 1)],
-                        rhs=b_words[g][:, cols].bitcast(FP8X4),
+                        rhs=b_words[g // B_LOAD][:, g % B_LOAD, cols].bitcast(FP8X4),
                         rhs_scale=b_planes[4 * (g % SHARED) : P, g // SHARED, cols],
                         start=(g == 0),
                         stop=(g == B_PASSES - 1),

@@ -27,11 +27,22 @@ N_TILE = 512
 CHUNK = 2048
 TILES_PER_CHUNK = CHUNK // N_TILE
 A_LOAD = 4096
-B_LOAD = 4
+B_TILE = 4
+B_TAIL = 14
+B_LOADS = [
+    (0, 4, 0, 2048),
+    (4, 4, 0, 2048),
+    (8, 4, 0, 2048),
+    (12, 2, 0, 2048),
+    (B_TAIL, 2, 0, 1024),
+    (B_TAIL, 2, 1024, 512),
+    (B_TAIL, 2, 1536, 512),
+]
 QUADRANT = 32
 SHARED = 4
 WORD_BUFS = 4
 GROUP_RUN = 4
+STORES = [(0, 1), (2,), (3,)]
 BANK_BUFS = 6
 
 ROW_A_BIAS = 0
@@ -212,15 +223,16 @@ def tile_mla_pa_k_kernel(
                 )
 
         b_words = []
-        for first in range(0, B_PASSES, B_LOAD):
-            words = word_pool.tile([P, B_LOAD, KV], U32, tag="words", align_bytes=64)
-            step = B_LOAD if first + B_LOAD < B_PASSES else 1
-            for k in range(0, B_LOAD, step):
-                nc.sync.dma_start(
-                    out=words[:, k : k + step, :].bitcast(I32),
-                    in_=wkv_b_w_words[first + k : first + k + step].rearrange("g p n t -> p g (n t)").bitcast(I32),
-                )
-            b_words.append(words)
+        for first, passes, col, width in B_LOADS:
+            if first % B_TILE == 0:
+                words = word_pool.tile([P, B_TILE, KV], U32, tag="words", align_bytes=64)
+                b_words.append(words)
+            slot = first % B_TILE
+            flat = wkv_b_w_words[first : first + passes].rearrange("g p n t -> p g (n t)")
+            nc.sync.dma_start(
+                out=b_words[first // B_TILE][:, slot : slot + passes, col : col + width].bitcast(I32),
+                in_=flat[:, :, PACK * col : PACK * (col + width)].bitcast(I32),
+            )
 
         total = const.tile([P, 1], F32)
         mean_eps = const.tile([P, 1], F32)
@@ -243,6 +255,19 @@ def tile_mla_pa_k_kernel(
         kv_codes = const.tile([P, B_PASSES * P], U32, align_bytes=64)
         kv_scales = const.tile([P, B_PASSES * P], U8, align_bytes=64)
         kv_ps = [psum.tile([P, N_TILE], F32, tag="mx", name="kv_ps%d" % i) for i in range(KV // N_TILE)]
+
+        def kv_pass(g, i):
+            cols = slice(N_TILE * i, N_TILE * (i + 1))
+            nc.tensor.matmul_mx(
+                out=kv_ps[i][:],
+                lhsT=kv_codes[:, P * g : P * (g + 1)].bitcast(FP8X4),
+                lhsT_scale=kv_scales[:, P * g : P * (g + 1)],
+                rhs=b_words[g // B_TILE][:, g % B_TILE, cols].bitcast(FP8X4),
+                rhs_scale=b_planes[4 * (g % SHARED) : P, g // SHARED, cols],
+                start=(g == 0),
+                stop=(g == B_PASSES - 1),
+            )
+
         for first in range(0, B_PASSES, GROUP_RUN):
             kv_grouped = work.tile([P, GROUP_RUN, P, PACK], BF16, align_bytes=64)
             nc.vector.tensor_tensor(
@@ -256,30 +281,26 @@ def tile_mla_pa_k_kernel(
                 scales=kv_scales[:, P * first : P * (first + GROUP_RUN)],
                 in_=kv_grouped[:].rearrange("p g m t -> p (g m t)"),
             )
-            for g in range(first, first + GROUP_RUN):
+            for g in range(first, min(first + GROUP_RUN, B_TAIL)):
                 for i in range(KV // N_TILE):
-                    cols = slice(N_TILE * i, N_TILE * (i + 1))
-                    nc.tensor.matmul_mx(
-                        out=kv_ps[i][:],
-                        lhsT=kv_codes[:, P * g : P * (g + 1)].bitcast(FP8X4),
-                        lhsT_scale=kv_scales[:, P * g : P * (g + 1)],
-                        rhs=b_words[g // B_LOAD][:, g % B_LOAD, cols].bitcast(FP8X4),
-                        rhs_scale=b_planes[4 * (g % SHARED) : P, g // SHARED, cols],
-                        start=(g == 0),
-                        stop=(g == B_PASSES - 1),
-                    )
+                    kv_pass(g, i)
+        for i in range(KV // N_TILE):
+            for g in range(B_TAIL, B_PASSES):
+                kv_pass(g, i)
 
         k_rows = out_0.rearrange("b s h d -> (b s) h d")
         v_rows = out_1.rearrange("b s h d -> (b s) h d")
         heads_per_bank = N_TILE // (2 * HEAD_DIM)
-        for i in range(KV // N_TILE):
-            heads = slice(heads_per_bank * i, heads_per_bank * (i + 1))
-            kv_out = banks.tile([P, 2, heads_per_bank, HEAD_DIM], F32, tag="bank")
-            nc.vector.tensor_tensor(
-                out=kv_out[:],
-                in0=kv_ps[i][:].rearrange("m (h s d) -> m s h d", s=2, d=HEAD_DIM),
-                in1=b_bias[:, i, :].rearrange("m (h s d) -> m s h d", s=2, d=HEAD_DIM),
-                op=ALU.add,
-            )
-            nc.sync.dma_start(out=k_rows[:, heads, :], in_=kv_out[:, 0])
-            nc.sync.dma_start(out=v_rows[:, heads, :], in_=kv_out[:, 1])
+        for stored in STORES:
+            heads = slice(heads_per_bank * stored[0], heads_per_bank * (stored[-1] + 1))
+            halves = [banks.tile([P, len(stored) * heads_per_bank, HEAD_DIM], F32, tag="bank", name="kv_out%d" % s) for s in range(2)]
+            for n, i in enumerate(stored):
+                for s in range(2):
+                    nc.vector.tensor_tensor(
+                        out=halves[s][:, heads_per_bank * n : heads_per_bank * (n + 1), :],
+                        in0=kv_ps[i][:].rearrange("m (h s d) -> m s h d", s=2, d=HEAD_DIM)[:, s],
+                        in1=b_bias[:, i, :].rearrange("m (h s d) -> m s h d", s=2, d=HEAD_DIM)[:, s],
+                        op=ALU.add,
+                    )
+            nc.sync.dma_start(out=k_rows[:, heads, :], in_=halves[0][:])
+            nc.scalar.dma_start(out=v_rows[:, heads, :], in_=halves[1][:])

@@ -32,11 +32,13 @@ B_TAIL = 14
 B_LOADS = [
     (0, 4, 0, 2048),
     (4, 4, 0, 2048),
-    (8, 4, 0, 2048),
+    (8, 2, 0, 2048),
+    (10, 2, 0, 2048),
     (12, 2, 0, 2048),
     (B_TAIL, 2, 0, 1024),
     (B_TAIL, 2, 1024, 512),
-    (B_TAIL, 2, 1536, 512),
+    (B_TAIL, 1, 1536, 512),
+    (B_TAIL + 1, 1, 1536, 512),
 ]
 QUADRANT = 32
 SHARED = 4
@@ -303,4 +305,4 @@ def tile_mla_pa_k_kernel(
                         op=ALU.add,
                     )
             nc.sync.dma_start(out=k_rows[:, heads, :], in_=halves[0][:])
-            nc.scalar.dma_start(out=v_rows[:, heads, :], in_=halves[1][:])
+            nc.sync.dma_start(out=v_rows[:, heads, :], in_=halves[1][:])

from contextlib import ExitStack

import concourse.mybir as mybir
from concourse.masks import make_identity

F32 = mybir.dt.float32
BF16 = mybir.dt.bfloat16
I32 = mybir.dt.int32
U32 = mybir.dt.uint32
U8 = mybir.dt.uint8
FP8X4 = mybir.dt.float8_e4m3fn_x4
ALU = mybir.AluOpType
ACT = mybir.ActivationFunctionType
AXIS = mybir.AxisListType

P = 128
PACK = 4
K_PASS = P * PACK
DIM = 1024
LATENT = 8192
KV = 2048
HEAD_DIM = 64
EPS = 1e-6
A_PASSES = DIM // K_PASS
B_PASSES = LATENT // K_PASS
N_TILE = 512
CHUNK = 2048
TILES_PER_CHUNK = CHUNK // N_TILE
A_LOAD = 4096
B_TILE = 4
B_TAIL = 14
B_LOADS = [
    (0, 4, 0, 2048),
    (4, 4, 0, 2048),
    (8, 2, 0, 2048),
    (10, 2, 0, 2048),
    (12, 2, 0, 2048),
    (B_TAIL, 2, 0, 1024),
    (B_TAIL, 2, 1024, 512),
    (B_TAIL, 1, 1536, 512),
    (B_TAIL + 1, 1, 1536, 512),
]
QUADRANT = 32
SHARED = 4
WORD_BUFS = 4
GROUP_RUN = 4
STORES = [(0, 1), (2,), (3,)]
BANK_BUFS = 6

ROW_A_BIAS = 0
ROW_GAIN = 16
ROW_B_BIAS = 32

FLOPS = 2 * P * (DIM * LATENT + LATENT * KV)


def load_shared_planes(queue, word, planes, scale_rows):
    for quad in range(4):
        first = QUADRANT * quad
        queue.dma_start(
            out=planes[first : first + 4 * SHARED, :].bitcast(word),
            in_=scale_rows[:, 4 * quad : 4 * quad + 4, :].bitcast(word),
        )


def broadcast_rows(nc, psum, ident_bf16, rows, first_row, dest):
    for j in range(0, dest.shape[1], 2):
        bank = psum.tile([P, 2, N_TILE], BF16, tag="plain")
        for i in range(2):
            row = first_row + j + i
            nc.tensor.matmul(
                out=bank[:, i, :],
                lhsT=ident_bf16[:, row : row + 1].to_broadcast([P, P]),
                rhs=rows,
                start=True,
                stop=True,
            )
        if j % 4 == 0:
            nc.vector.tensor_copy(out=dest[:, j : j + 2, :], in_=bank[:])
        else:
            nc.scalar.copy(out=dest[:, j : j + 2, :], in_=bank[:])


def tile_mla_pa_k_kernel(
    tc,
    x,
    wkv_a_w_words,
    wkv_a_w_scales,
    wkv_a_b,
    kv_norm_w,
    wkv_b_w_words,
    wkv_b_w_scales,
    wkv_b_b,
    out_0,
    out_1,
):
    nc = tc.nc
    with ExitStack() as ctx:
        const = ctx.enter_context(tc.tile_pool(name="const", bufs=1))
        word_pool = ctx.enter_context(tc.tile_pool(name="word_pool", bufs=WORD_BUFS))
        work = ctx.enter_context(tc.tile_pool(name="work", bufs=2))
        banks = ctx.enter_context(tc.tile_pool(name="banks", bufs=BANK_BUFS))
        psum = ctx.enter_context(tc.psum_pool(name="psum", bufs=4))

        rows = const.tile([P, N_TILE], BF16)
        a_planes = const.tile([P, A_PASSES, CHUNK], U8, align_bytes=64)
        b_planes = const.tile([P, B_PASSES // SHARED, KV], U8, align_bytes=64)
        nc.vector.memset(rows[:], 0.0)
        nc.vector.memset(a_planes[:].bitcast(I32), 0)
        nc.vector.memset(b_planes[:].bitcast(I32), 0)

        ident_f32 = const.tile([P, P], F32)
        ident_bf16 = const.tile([P, P], BF16)
        make_identity(nc, ident_f32[:])
        make_identity(nc, ident_bf16[:])

        nc.scalar.dma_start(
            out=rows[ROW_A_BIAS : ROW_A_BIAS + LATENT // N_TILE, :],
            in_=wkv_a_b.rearrange("(r c) -> r c", c=N_TILE),
        )
        nc.scalar.dma_start(
            out=rows[ROW_GAIN : ROW_GAIN + LATENT // N_TILE, :],
            in_=kv_norm_w.rearrange("(r c) -> r c", c=N_TILE),
        )
        nc.scalar.dma_start(
            out=rows[ROW_B_BIAS : ROW_B_BIAS + KV // N_TILE, :],
            in_=wkv_b_b.rearrange("(r c) -> r c", c=N_TILE),
        )
        for block in range(B_PASSES // SHARED):
            load_shared_planes(
                nc.gpsimd, F32, b_planes[:, block, :], wkv_b_w_scales[SHARED * block : SHARED * (block + 1)]
            )
        x_sb = const.tile([P, DIM], BF16)
        nc.sync.dma_start(out=x_sb[:], in_=x.flatten_outer_dims())
        a_words = []
        for h in range(LATENT // A_LOAD):
            words = word_pool.tile([P, A_PASSES, A_LOAD], U32, tag="words", align_bytes=64)
            for g in range(A_PASSES):
                if h == 0:
                    load_shared_planes(
                        nc.sync, I32, a_planes[:, g, :], wkv_a_w_scales[g].rearrange("q (j c) -> j q c", j=SHARED)
                    )
                flat = wkv_a_w_words[g].rearrange("p n t -> p (n t)")
                nc.sync.dma_start(
                    out=words[:, g, :].bitcast(I32),
                    in_=flat[:, PACK * A_LOAD * h : PACK * A_LOAD * (h + 1)].bitcast(I32),
                )
            a_words.append(words)

        x_words = x_sb[:].bitcast(F32)
        x_t = psum.tile([P, A_PASSES, 2, P], F32, tag="plain")
        for g in range(A_PASSES):
            for u in range(2):
                nc.tensor.transpose(
                    x_t[:, g, u, :],
                    x_words[:, (K_PASS // 2) * g + u : (K_PASS // 2) * (g + 1) : 2],
                    ident_f32[:],
                )
        x_grouped = const.tile([P, A_PASSES * P * PACK], BF16, align_bytes=64)
        nc.vector.tensor_copy(
            out=x_grouped[:].bitcast(F32).rearrange("p (g m u) -> p g m u", g=A_PASSES, u=2),
            in_=x_t[:].rearrange("p g u m -> p g m u"),
        )
        x_codes = const.tile([P, A_PASSES * P], U32, align_bytes=64)
        x_scales = const.tile([P, A_PASSES * P], U8, align_bytes=64)
        nc.vector.quantize_mx(out=x_codes[:].bitcast(FP8X4), scales=x_scales[:], in_=x_grouped[:])

        rows_tp = const.tile([P, PACK, P], BF16)
        nc.vector.tensor_copy(out=rows_tp[:], in_=rows[:].rearrange("r (p t) -> r t p", t=PACK))
        a_bias = const.tile([P, B_PASSES, N_TILE], BF16)
        broadcast_rows(
            nc, psum, ident_bf16, rows_tp[:].rearrange("r t p -> r (t p)"), ROW_A_BIAS, a_bias
        )
        rows_t = psum.tile([P, PACK, P], BF16, tag="plain")
        for t in range(PACK):
            nc.tensor.transpose(rows_t[:, t, :], rows_tp[:, t, :], ident_bf16[:])
        gain = const.tile([P, B_PASSES, PACK], F32)
        nc.vector.tensor_copy(
            out=gain[:], in_=rows_t[:, :, ROW_GAIN : ROW_GAIN + B_PASSES].rearrange("p t g -> p g t")
        )

        c_gain = const.tile([P, B_PASSES, P, PACK], F32)
        sum_sq = const.tile([P, B_PASSES], F32)
        for j in range(LATENT // CHUNK):
            c_ps = [psum.tile([P, N_TILE], F32, tag="mx", name="c_ps%d" % i) for i in range(TILES_PER_CHUNK)]
            for g in range(A_PASSES):
                for i in range(TILES_PER_CHUNK):
                    cols = slice(N_TILE * i, N_TILE * (i + 1))
                    first_word = (CHUNK * j) % A_LOAD + N_TILE * i
                    word_cols = slice(first_word, first_word + N_TILE)
                    nc.tensor.matmul_mx(
                        out=c_ps[i][:],
                        lhsT=x_codes[:, P * g : P * (g + 1)].bitcast(FP8X4),
                        lhsT_scale=x_scales[:, P * g : P * (g + 1)],
                        rhs=a_words[CHUNK * j // A_LOAD][:, g, word_cols].bitcast(FP8X4),
                        rhs_scale=a_planes[4 * j : P, g, cols],
                        start=(g == 0),
                        stop=(g == A_PASSES - 1),
                    )
            c_sb = []
            for i in range(TILES_PER_CHUNK):
                bank_no = TILES_PER_CHUNK * j + i
                c_bank = banks.tile([P, PACK, P], F32, tag="bank")
                nc.vector.tensor_tensor(
                    out=c_bank[:],
                    in0=c_ps[i][:].rearrange("m (p t) -> m t p", t=PACK),
                    in1=a_bias[:, bank_no, :].rearrange("m (t p) -> m t p", t=PACK),
                    op=ALU.add,
                )
                squares = work.tile([P, PACK, P], BF16)
                nc.scalar.activation(
                    out=squares[:], in_=c_bank[:], func=ACT.Square, accum_out=sum_sq[:, bank_no : bank_no + 1]
                )
                c_sb.append(c_bank)
            for i in range(TILES_PER_CHUNK):
                bank_no = TILES_PER_CHUNK * j + i
                c_t = psum.tile([P, PACK, P], F32, tag="plain")
                for t in range(PACK):
                    nc.tensor.transpose(c_t[:, t, :], c_sb[i][:, t, :], ident_f32[:])
                nc.vector.tensor_tensor(
                    out=c_gain[:, bank_no],
                    in0=c_t[:].rearrange("p t m -> p m t"),
                    in1=gain[:, bank_no, :].unsqueeze(1).to_broadcast([P, P, PACK]),
                    op=ALU.mult,
                )

        b_words = []
        for first, passes, col, width in B_LOADS:
            if first % B_TILE == 0:
                words = word_pool.tile([P, B_TILE, KV], U32, tag="words", align_bytes=64)
                b_words.append(words)
            slot = first % B_TILE
            flat = wkv_b_w_words[first : first + passes].rearrange("g p n t -> p g (n t)")
            nc.sync.dma_start(
                out=b_words[first // B_TILE][:, slot : slot + passes, col : col + width].bitcast(I32),
                in_=flat[:, :, PACK * col : PACK * (col + width)].bitcast(I32),
            )

        total = const.tile([P, 1], F32)
        mean_eps = const.tile([P, 1], F32)
        rms = const.tile([P, 1], F32)
        inv_rms = const.tile([P, 1], F32)
        nc.vector.reduce_sum(out=total[:], in_=sum_sq[:], axis=AXIS.X)
        nc.vector.tensor_scalar(
            out=mean_eps[:], in0=total[:], scalar1=1.0 / LATENT, scalar2=EPS, op0=ALU.mult, op1=ALU.add
        )
        nc.scalar.sqrt(out=rms[:], in_=mean_eps[:])
        nc.vector.reciprocal(out=inv_rms[:], in_=rms[:])
        inv_rms_rep = const.tile([P, P], F32)
        nc.vector.tensor_copy(out=inv_rms_rep[:], in_=inv_rms[:, 0:1].to_broadcast([P, P]))
        inv_rms_t = psum.tile([P, P], F32, tag="plain")
        nc.tensor.transpose(inv_rms_t[:], inv_rms_rep[:], ident_f32[:])

        b_bias = const.tile([P, KV // N_TILE, N_TILE], BF16)
        broadcast_rows(nc, psum, ident_bf16, rows[:], ROW_B_BIAS, b_bias)

        kv_codes = const.tile([P, B_PASSES * P], U32, align_bytes=64)
        kv_scales = const.tile([P, B_PASSES * P], U8, align_bytes=64)
        kv_ps = [psum.tile([P, N_TILE], F32, tag="mx", name="kv_ps%d" % i) for i in range(KV // N_TILE)]

        def kv_pass(g, i):
            cols = slice(N_TILE * i, N_TILE * (i + 1))
            nc.tensor.matmul_mx(
                out=kv_ps[i][:],
                lhsT=kv_codes[:, P * g : P * (g + 1)].bitcast(FP8X4),
                lhsT_scale=kv_scales[:, P * g : P * (g + 1)],
                rhs=b_words[g // B_TILE][:, g % B_TILE, cols].bitcast(FP8X4),
                rhs_scale=b_planes[4 * (g % SHARED) : P, g // SHARED, cols],
                start=(g == 0),
                stop=(g == B_PASSES - 1),
            )

        for first in range(0, B_PASSES, GROUP_RUN):
            kv_grouped = work.tile([P, GROUP_RUN, P, PACK], BF16, align_bytes=64)
            nc.vector.tensor_tensor(
                out=kv_grouped[:],
                in0=c_gain[:, first : first + GROUP_RUN],
                in1=inv_rms_t[:].unsqueeze(1).unsqueeze(3).to_broadcast([P, GROUP_RUN, P, PACK]),
                op=ALU.mult,
            )
            nc.vector.quantize_mx(
                out=kv_codes[:, P * first : P * (first + GROUP_RUN)].bitcast(FP8X4),
                scales=kv_scales[:, P * first : P * (first + GROUP_RUN)],
                in_=kv_grouped[:].rearrange("p g m t -> p (g m t)"),
            )
            for g in range(first, min(first + GROUP_RUN, B_TAIL)):
                for i in range(KV // N_TILE):
                    kv_pass(g, i)
        for i in range(KV // N_TILE):
            for g in range(B_TAIL, B_PASSES):
                kv_pass(g, i)

        k_rows = out_0.rearrange("b s h d -> (b s) h d")
        v_rows = out_1.rearrange("b s h d -> (b s) h d")
        heads_per_bank = N_TILE // (2 * HEAD_DIM)
        for stored in STORES:
            heads = slice(heads_per_bank * stored[0], heads_per_bank * (stored[-1] + 1))
            halves = [banks.tile([P, len(stored) * heads_per_bank, HEAD_DIM], F32, tag="bank", name="kv_out%d" % s) for s in range(2)]
            for n, i in enumerate(stored):
                for s in range(2):
                    nc.vector.tensor_tensor(
                        out=halves[s][:, heads_per_bank * n : heads_per_bank * (n + 1), :],
                        in0=kv_ps[i][:].rearrange("m (h s d) -> m s h d", s=2, d=HEAD_DIM)[:, s],
                        in1=b_bias[:, i, :].rearrange("m (h s d) -> m s h d", s=2, d=HEAD_DIM)[:, s],
                        op=ALU.add,
                    )
            nc.sync.dma_start(out=k_rows[:, heads, :], in_=halves[0][:])
            nc.sync.dma_start(out=v_rows[:, heads, :], in_=halves[1][:])
